import numpy as np
import ml_dtypes


def mxq(x, axis, fmt="e4m3"):
    dtype, down = {"e4m3": (ml_dtypes.float8_e4m3fn, 7), "e5m2": (ml_dtypes.float8_e5m2, 14)}[fmt]
    v = np.moveaxis(np.asarray(x, np.float32).astype(ml_dtypes.bfloat16).astype(np.float64), axis, -1)
    blocks = v.reshape(v.shape[:-1] + (-1, 32))
    amax = np.abs(blocks).max(-1, keepdims=True)
    byte = np.maximum(np.where(amax > 0, np.frexp(amax)[1] - 1 + 127, 0) - down, 1)
    scale = np.exp2(byte - 127.0)
    codes = (blocks / scale).astype(np.float32).astype(dtype).astype(np.float64)
    return np.moveaxis((codes * scale).reshape(v.shape), -1, axis)


WIDE = False


def mx_kscale(k):
    if not WIDE:
        return np.ones(k)
    levels = np.array([10, -10, 5, -5, 0])
    a = np.random.permutation(np.resize(levels, k // 512 * 4)).reshape(k // 512, 4)
    idx = np.arange(k)
    return np.exp2(a[idx // 512, idx % 128 // 32])


BF16 = ml_dtypes.bfloat16


def bf(x):
    return np.asarray(x, np.float32).astype(BF16)


def f64(x):
    return np.asarray(x).astype(np.float64)


E2M1 = np.array([0.0, 0.5, 1.0, 1.5, 2.0, 3.0, 4.0, 6.0, -0.0, -0.5, -1.0, -1.5, -2.0, -3.0, -4.0, -6.0])


def pack_weight(w, fmt):
    k, n = w.shape
    w = f64(bf(w)).reshape(k // 32, 32, n)
    amax = np.abs(w).max(1)
    if fmt == "e4m3":
        byte = np.frexp(amax)[1] - 1 + 127 - 7
    else:
        mant, ex = np.frexp(amax / 6.0)
        byte = np.where(mant > 0.5, ex, ex - 1) + 127
    byte = np.clip(np.where(amax > 0, byte, 1), 1, 254)
    scaled = (w * np.exp2(127.0 - byte)[:, None, :]).reshape(k, n).astype(np.float32)
    by_word = np.ascontiguousarray(scaled.reshape(k // 512, 128, 4, n).transpose(0, 1, 3, 2))
    if fmt == "e4m3":
        words = by_word.astype(ml_dtypes.float8_e4m3fn).view(np.uint8)
    else:
        c = by_word.astype(ml_dtypes.float4_e2m1fn).view(np.uint8) & 0xF
        words = c[..., 0::2] | (c[..., 1::2] << 4)
    return np.ascontiguousarray(words), np.ascontiguousarray(byte.astype(np.uint8).reshape(k // 512, 16, n))


def unpack_weight(words, scales, fmt):
    g, p, n, _ = words.shape
    if fmt == "e4m3":
        vals = np.ascontiguousarray(words).view(ml_dtypes.float8_e4m3fn).astype(np.float64)
    else:
        nib = np.empty((g, p, n, 4), np.uint8)
        nib[..., 0::2] = words & 0xF
        nib[..., 1::2] = words >> 4
        vals = E2M1[nib]
    vals = vals * np.repeat(np.exp2(scales.astype(np.float64) - 127.0), 8, axis=1)[..., None]
    return vals.transpose(0, 1, 3, 2).reshape(g * 512, n)


B, K, N = 128, 4608, 4608


def setup_inputs():
    s = mx_kscale(K)
    s = s / s.max()
    x = bf(np.random.standard_normal((B, K)) * s)
    W_words, W_scales = pack_weight(np.random.standard_normal((K, N)) * 0.4 / np.sqrt(K) / s[:, None], "e4m3")
    return {"x": x,
            "W_words": W_words,
            "W_scales": W_scales,
            "P": bf(np.random.standard_normal(N) * 0.3),
            "w": bf(0.8 + 0.1 * np.random.standard_normal(1)),
            "p": bf(0.5 + 0.1 * np.random.standard_normal(1)),
            "sine_w": bf(1.2 + 0.1 * np.random.standard_normal(1)),
            "cosine_w": bf(-0.7 + 0.1 * np.random.standard_normal(1))}


def reference(x, W_words, W_scales, P, w, p, sine_w, cosine_w):
    x = f64(x)
    original = f64(w) * x + f64(p)
    z = (mxq(x, 1, "e4m3") @ unpack_weight(W_words, W_scales, "e4m3")) + f64(P)
    periodic = f64(sine_w) * np.sin(z) + f64(cosine_w) * np.cos(z)
    return np.concatenate((original, periodic), axis=-1)

@@ -1,0 +1,222 @@
+import math
+from contextlib import ExitStack
+
+import concourse.bass as bass
+import concourse.mybir as mybir
+import concourse.tile as tile
+from concourse.masks import make_identity
+
+F32 = mybir.dt.float32
+BF16 = mybir.dt.bfloat16
+I32 = mybir.dt.int32
+U32 = mybir.dt.uint32
+U8 = mybir.dt.uint8
+FP8X4 = mybir.dt.float8_e4m3fn_x4
+ALU = mybir.AluOpType
+ACT = mybir.ActivationFunctionType
+
+B = 128
+K = 4608
+N = 4608
+GROUPS = K // 512
+FLOPS = 2 * B * K * N
+
+PIN = True
+TEST_ROUND = False
+SCALES_ON_GPSIMD = False
+ROUNDS = ((0, 2048), (2048, 1536), (3584, 1024))
+W_MAX = 2048
+W_BUFS = 12
+TURNS = 3.0 if TEST_ROUND else 0.0
+
+
+def tile_time2vec_w_kernel(tc, x, W_words, W_scales, P, w, p, sine_w, cosine_w, out):
+    nc = tc.nc
+    with ExitStack() as ctx:
+        keep = ctx.enter_context(tc.tile_pool(name="keep", bufs=1))
+        wpool = ctx.enter_context(tc.tile_pool(name="wpool", bufs=W_BUFS))
+        work = ctx.enter_context(tc.tile_pool(name="work", bufs=3))
+        psum = ctx.enter_context(tc.psum_pool(name="psum", bufs=8))
+        if PIN:
+            ctx.enter_context(tc.manual_schedule())
+
+        x_sb = keep.tile([B, K], BF16, align_bytes=64)
+        nc.sync.dma_start(out=x_sb[:], in_=x[:, :])
+
+        planes_a = keep.tile([128, N], U8, align_bytes=64)
+        planes_b = keep.tile([128, N], U8, align_bytes=64)
+        planes_c = keep.tile([128, N // 3], U8, align_bytes=64)
+        nc.vector.memset(planes_a[:].bitcast(I32), 0)
+        nc.vector.memset(planes_b[:].bitcast(I32), 0)
+        nc.vector.memset(planes_c[:].bitcast(I32), 0)
+
+        prow = keep.tile([128, N + 64], BF16)
+        nc.vector.memset(prow[:], 0.0)
+        ones = keep.tile([128, 128], BF16)
+        nc.vector.memset(ones[:], 1.0)
+        ident = keep.tile([128, 128], F32)
+        make_identity(nc, ident[:])
+
+        for i, s in enumerate((w, p, sine_w, cosine_w)):
+            nc.scalar.dma_start(
+                out=prow[0:1, N + 16 * i : N + 16 * i + 1], in_=s.rearrange("(o n) -> o n", o=1)
+            )
+        nc.scalar.dma_start(out=prow[0:1, 0:N], in_=P.rearrange("(o n) -> o n", o=1))
+
+        view = F32 if SCALES_ON_GPSIMD else I32
+        queue = nc.gpsimd if SCALES_ON_GPSIMD else nc.sync
+        for planes, g0 in ((planes_a, 0), (planes_b, 4)):
+            for q in range(4):
+                queue.dma_start(
+                    out=planes[32 * q : 32 * q + 16, :].bitcast(view),
+                    in_=W_scales[g0 : g0 + 4, 4 * q : 4 * q + 4, :].bitcast(view),
+                )
+        for q in range(4):
+            queue.dma_start(
+                out=planes_c[32 * q : 32 * q + 12, :].bitcast(view),
+                in_=W_scales[8, 4 * q : 4 * q + 4, :].rearrange("r (k c) -> k r c", k=3).bitcast(view),
+            )
+
+        chunks = [(c0, width, g) for (c0, width) in ROUNDS for g in range(GROUPS)]
+        w_tiles = {}
+
+        def load_chunk(i):
+            c0, width, g = chunks[i]
+            wt = wpool.tile([128, 4 * W_MAX], U8, name="wt", tag="wt", align_bytes=64)
+            nc.sync.dma_start(
+                out=wt[:, 0 : 4 * width].bitcast(I32),
+                in_=W_words[g].rearrange("p n t -> p (n t)")[:, 4 * c0 : 4 * (c0 + width)].bitcast(I32),
+            )
+            w_tiles[i] = wt
+
+        for i in range(W_BUFS):
+            load_chunk(i)
+
+        xw = x_sb[:].bitcast(F32)
+        grouped = keep.tile([128, K], BF16, align_bytes=64)
+        g32 = grouped[:].bitcast(F32).rearrange("p (g b u) -> p g b u", g=GROUPS, b=B, u=2)
+        xcodes = keep.tile([128, GROUPS * B], U32, align_bytes=64)
+        xscales = keep.tile([128, GROUPS * B], U8, align_bytes=64)
+        pairs = [(g0, min(2, GROUPS - g0)) for g0 in range(0, GROUPS, 2)]
+
+        def quantise(g0, ng):
+            nc.vector.quantize_mx(
+                out=xcodes[:, B * g0 : B * (g0 + ng)].bitcast(FP8X4),
+                scales=xscales[:, B * g0 : B * (g0 + ng)],
+                in_=grouped[:, 512 * g0 : 512 * (g0 + ng)],
+            )
+
+        for n_pair, (g0, ng) in enumerate(pairs):
+            xt = psum.tile([128, 2, 2, B], F32, name="xt", tag="bank")
+            for j in range(ng):
+                for u in range(2):
+                    g = g0 + j
+                    nc.tensor.transpose(xt[:, j, u, :], xw[:, 256 * g + u : 256 * (g + 1) : 2], ident[:])
+            nc.vector.tensor_copy(
+                out=g32[:, g0 : g0 + ng], in_=xt[:, 0:ng].rearrange("p g u b -> p g b u")
+            )
+            if n_pair > 0:
+                quantise(*pairs[n_pair - 1])
+        quantise(*pairs[-1])
+
+        ps = psum.tile([128, 512], F32, name="ps", tag="bank")
+        nc.tensor.matmul(out=ps[:, 0:64], lhsT=ones[:], rhs=prow[:, N : N + 64], start=True, stop=True)
+        scal = keep.tile([128, 64], F32)
+        nc.vector.tensor_copy(out=scal[:], in_=ps[:, 0:64])
+        w_c = scal[:, 0:1]
+        p_c = scal[:, 16:17]
+        sw_c = scal[:, 32:33]
+        cw_c = scal[:, 48:49]
+        m2cw = keep.tile([128, 1], F32)
+        nc.vector.tensor_scalar_mul(out=m2cw[:], in0=cw_c, scalar1=-2.0)
+
+        pb = keep.tile([128, N], F32)
+        for j in range(N // 512):
+            ps = psum.tile([128, 512], F32, name="ps", tag="bank")
+            nc.tensor.matmul(
+                out=ps[:], lhsT=ones[:], rhs=prow[:, 512 * j : 512 * (j + 1)], start=True, stop=True
+            )
+            nc.scalar.activation(
+                out=pb[:, 512 * j : 512 * (j + 1)], in_=ps[:], func=ACT.Copy,
+                bias=TURNS, scale=1.0 / (2.0 * math.pi),
+            )
+
+        lin = keep.tile([128, K], F32)
+        for c in range(0, K, 1536):
+            nc.scalar.activation(
+                out=lin[:, c : c + 1536], in_=x_sb[:, c : c + 1536], func=ACT.Identity, bias=p_c, scale=w_c
+            )
+
+        per = keep.tile([128, N], F32)
+
+        def plane(g, col):
+            j = col // 512
+            if g < 4:
+                return planes_a[4 * g : 128, col : col + 512]
+            if g < 8:
+                return planes_b[4 * (g - 4) : 128, col : col + 512]
+            return planes_c[4 * (j // 3) : 128, 512 * (j % 3) : 512 * (j % 3) + 512]
+
+        def front(acc, col):
+            u = work.tile([128, 512], F32, name="u", tag="u")
+            nc.vector.scalar_tensor_tensor(
+                out=u[:], in0=acc[:], scalar=1.0 / (2.0 * math.pi), in1=pb[:, col : col + 512],
+                op0=ALU.mult, op1=ALU.add,
+            )
+            ki = work.tile([128, 512], I32, name="ki", tag="ki")
+            nc.vector.tensor_copy(out=ki[:], in_=u[:])
+            f = work.tile([128, 512], F32, name="f", tag="f")
+            nc.vector.tensor_tensor(out=f[:], in0=u[:], in1=ki[:], op=ALU.subtract)
+            s = work.tile([128, 512], F32, name="s", tag="s")
+            nc.scalar.activation(out=s[:], in_=f[:], func=ACT.Sin, scale=2.0 * math.pi)
+            h = work.tile([128, 512], F32, name="h", tag="h")
+            nc.scalar.activation(out=h[:], in_=f[:], func=ACT.Sin, scale=math.pi)
+            nc.scalar.activation(out=h[:], in_=h[:], func=ACT.Square)
+            return u, f, s, h
+
+        def back(col, u, f, s, h):
+            nc.vector.tensor_scalar(
+                out=h[:], in0=h[:], scalar1=m2cw[:, 0:1], scalar2=cw_c, op0=ALU.mult, op1=ALU.add
+            )
+            if TEST_ROUND:
+                nc.vector.scalar_tensor_tensor(
+                    out=u[:], in0=u[:], scalar=-TURNS, in1=f[:], op0=ALU.add, op1=ALU.subtract
+                )
+                nc.vector.tensor_tensor(out=h[:], in0=h[:], in1=u[:], op=ALU.add)
+            nc.vector.scalar_tensor_tensor(
+                out=per[:, col : col + 512], in0=s[:], scalar=sw_c, in1=h[:], op0=ALU.mult, op1=ALU.add
+            )
+
+        i = 0
+        for c0, width in ROUNDS:
+            cols = list(range(c0, c0 + width, 512))
+            accs = [psum.tile([128, 512], F32, name="acc", tag="bank") for col in cols]
+            for g in range(GROUPS):
+                wt = w_tiles[i]
+                for acc, col in zip(accs, cols):
+                    nc.tensor.matmul_mx(
+                        out=acc[:],
+                        lhsT=xcodes[:, B * g : B * (g + 1)].bitcast(FP8X4),
+                        lhsT_scale=xscales[:, B * g : B * (g + 1)],
+                        rhs=wt[:, 4 * (col - c0) : 4 * (col - c0) + 2048].bitcast(FP8X4),
+                        rhs_scale=plane(g, col),
+                        start=(g == 0),
+                        stop=(g == GROUPS - 1),
+                    )
+                if i + W_BUFS < len(chunks):
+                    load_chunk(i + W_BUFS)
+                i += 1
+            held = None
+            for acc, col in zip(accs, cols):
+                parts = front(acc, col)
+                if held is not None:
+                    back(*held)
+                held = (col,) + parts
+            back(*held)
+
+        nc.sync.dma_start(out=out[:, 0:K], in_=lin[:])
+        for c0, width in ROUNDS[:-1]:
+            nc.sync.dma_start(out=out[:, K + c0 : K + c0 + width], in_=per[:, c0 : c0 + width])
+        c0, width = ROUNDS[-1]
+        for col in range(c0, c0 + width, 512):
+            nc.sync.dma_start(out=out[:, K + col : K + col + 512], in_=per[:, col : col + 512])

@@ -1,9 +1,7 @@
 import math
 from contextlib import ExitStack
 
-import concourse.bass as bass
 import concourse.mybir as mybir
-import concourse.tile as tile
 from concourse.masks import make_identity
 
 F32 = mybir.dt.float32
@@ -21,13 +19,12 @@ N = 4608
 GROUPS = K // 512
 FLOPS = 2 * B * K * N
 
-PIN = True
-TEST_ROUND = False
-SCALES_ON_GPSIMD = False
-ROUNDS = ((0, 2048), (2048, 1536), (3584, 1024))
-W_MAX = 2048
-W_BUFS = 12
-TURNS = 3.0 if TEST_ROUND else 0.0
+ROUNDS = ((0, 3072), (3072, 1536))
+W_MAX = 3072
+W_BUFS = 8
+BUNCH = 3
+NEWTON = 4
+TWO_PI = 2.0 * math.pi
 
 
 def tile_time2vec_w_kernel(tc, x, W_words, W_scales, P, w, p, sine_w, cosine_w, out):
@@ -35,23 +32,21 @@ def tile_time2vec_w_kernel(tc, x, W_words, W_scales, P, w, p, sine_w, cosine_w, 
     with ExitStack() as ctx:
         keep = ctx.enter_context(tc.tile_pool(name="keep", bufs=1))
         wpool = ctx.enter_context(tc.tile_pool(name="wpool", bufs=W_BUFS))
-        work = ctx.enter_context(tc.tile_pool(name="work", bufs=3))
+        work = ctx.enter_context(tc.tile_pool(name="work", bufs=4))
         psum = ctx.enter_context(tc.psum_pool(name="psum", bufs=8))
-        if PIN:
-            ctx.enter_context(tc.manual_schedule())
+        ctx.enter_context(tc.manual_schedule())
 
         x_sb = keep.tile([B, K], BF16, align_bytes=64)
         nc.sync.dma_start(out=x_sb[:], in_=x[:, :])
 
+        prow = keep.tile([128, N + 64], BF16)
+        nc.vector.memset(prow[:], 0.0)
         planes_a = keep.tile([128, N], U8, align_bytes=64)
         planes_b = keep.tile([128, N], U8, align_bytes=64)
         planes_c = keep.tile([128, N // 3], U8, align_bytes=64)
         nc.vector.memset(planes_a[:].bitcast(I32), 0)
         nc.vector.memset(planes_b[:].bitcast(I32), 0)
         nc.vector.memset(planes_c[:].bitcast(I32), 0)
-
-        prow = keep.tile([128, N + 64], BF16)
-        nc.vector.memset(prow[:], 0.0)
         ones = keep.tile([128, 128], BF16)
         nc.vector.memset(ones[:], 1.0)
         ident = keep.tile([128, 128], F32)
@@ -63,18 +58,16 @@ def tile_time2vec_w_kernel(tc, x, W_words, W_scales, P, w, p, sine_w, cosine_w, 
             )
         nc.scalar.dma_start(out=prow[0:1, 0:N], in_=P.rearrange("(o n) -> o n", o=1))
 
-        view = F32 if SCALES_ON_GPSIMD else I32
-        queue = nc.gpsimd if SCALES_ON_GPSIMD else nc.sync
         for planes, g0 in ((planes_a, 0), (planes_b, 4)):
             for q in range(4):
-                queue.dma_start(
-                    out=planes[32 * q : 32 * q + 16, :].bitcast(view),
-                    in_=W_scales[g0 : g0 + 4, 4 * q : 4 * q + 4, :].bitcast(view),
+                nc.sync.dma_start(
+                    out=planes[32 * q : 32 * q + 16, :].bitcast(I32),
+                    in_=W_scales[g0 : g0 + 4, 4 * q : 4 * q + 4, :].bitcast(I32),
                 )
         for q in range(4):
-            queue.dma_start(
-                out=planes_c[32 * q : 32 * q + 12, :].bitcast(view),
-                in_=W_scales[8, 4 * q : 4 * q + 4, :].rearrange("r (k c) -> k r c", k=3).bitcast(view),
+            nc.sync.dma_start(
+                out=planes_c[32 * q : 32 * q + 12, :].bitcast(I32),
+                in_=W_scales[8, 4 * q : 4 * q + 4, :].rearrange("r (k c) -> k r c", k=3).bitcast(I32),
             )
 
         chunks = [(c0, width, g) for (c0, width) in ROUNDS for g in range(GROUPS)]
@@ -121,32 +114,87 @@ def tile_time2vec_w_kernel(tc, x, W_words, W_scales, P, w, p, sine_w, cosine_w, 
 
         ps = psum.tile([128, 512], F32, name="ps", tag="bank")
         nc.tensor.matmul(out=ps[:, 0:64], lhsT=ones[:], rhs=prow[:, N : N + 64], start=True, stop=True)
-        scal = keep.tile([128, 64], F32)
-        nc.vector.tensor_copy(out=scal[:], in_=ps[:, 0:64])
-        w_c = scal[:, 0:1]
-        p_c = scal[:, 16:17]
-        sw_c = scal[:, 32:33]
-        cw_c = scal[:, 48:49]
-        m2cw = keep.tile([128, 1], F32)
-        nc.vector.tensor_scalar_mul(out=m2cw[:], in0=cw_c, scalar1=-2.0)
+        sc4 = keep.tile([128, 4], F32)
+        nc.vector.tensor_copy(out=sc4[:], in_=ps[:, 0:64:16])
+        w_c = sc4[:, 0:1]
+        p_c = sc4[:, 1:2]
+        sw_c = sc4[:, 2:3]
+        cw_c = sc4[:, 3:4]
+
+        def small(name, width=1):
+            return keep.tile([128, width], F32, name=name)
+
+        mag = small("mag", 2)
+        nc.vector.scalar_tensor_tensor(
+            out=mag[:], in0=sc4[:, 2:4], scalar=-1.0, in1=sc4[:, 2:4], op0=ALU.mult, op1=ALU.max
+        )
+        big = small("big")
+        nc.vector.scalar_tensor_tensor(
+            out=big[:], in0=mag[:, 0:1], scalar=1e-30, in1=mag[:, 1:2], op0=ALU.max, op1=ALU.max
+        )
+        rbig = small("rbig")
+        nc.vector.reciprocal(out=rbig[:], in_=big[:])
+        vec = small("vec", 2)
+        nc.vector.tensor_scalar_mul(out=vec[:, 0:1], in0=sw_c, scalar1=rbig[:, 0:1])
+        nc.vector.tensor_scalar_mul(out=vec[:, 1:2], in0=mag[:, 1:2], scalar1=rbig[:, 0:1])
+        sq = small("sq", 2)
+        nc.vector.tensor_tensor(out=sq[:], in0=vec[:], in1=vec[:], op=ALU.mult)
+        n2 = small("n2")
+        nc.vector.tensor_scalar(
+            out=n2[:], in0=sq[:, 0:1], scalar1=sq[:, 1:2], scalar2=0.25, op0=ALU.add, op1=ALU.max
+        )
+        root = small("root")
+        nc.scalar.activation(out=root[:], in_=n2[:], func=ACT.Sqrt)
+        rroot = small("rroot")
+        nc.vector.reciprocal(out=rroot[:], in_=root[:])
+        twice = small("twice")
+        nc.vector.tensor_scalar(
+            out=twice[:], in0=n2[:], scalar1=rroot[:, 0:1], scalar2=root[:, 0:1], op0=ALU.mult, op1=ALU.add
+        )
+        amp = small("amp")
+        nc.vector.tensor_scalar(
+            out=amp[:], in0=twice[:], scalar1=0.5, scalar2=big[:, 0:1], op0=ALU.mult, op1=ALU.mult
+        )
+        neg_cos = small("neg_cos")
+        nc.vector.tensor_scalar(
+            out=neg_cos[:], in0=vec[:, 0:1], scalar1=rroot[:, 0:1], scalar2=-1.0, op0=ALU.mult, op1=ALU.mult
+        )
+        pos_sin = small("pos_sin")
+        nc.vector.tensor_scalar_mul(out=pos_sin[:], in0=vec[:, 1:2], scalar1=rroot[:, 0:1])
+        psi = small("psi")
+        nc.vector.memset(psi[:], math.pi / 2.0)
+        trig = small("trig", 2)
+        for step in range(NEWTON):
+            nc.scalar.activation(out=trig[:, 0:1], in_=psi[:], func=ACT.Sin)
+            nc.scalar.activation(out=trig[:, 1:2], in_=psi[:], func=ACT.Sin, bias=math.pi / 2.0, scale=-1.0)
+            nc.vector.scalar_tensor_tensor(
+                out=psi[:], in0=trig[:, 0:1], scalar=neg_cos[:, 0:1], in1=psi[:], op0=ALU.mult, op1=ALU.add
+            )
+            nc.vector.scalar_tensor_tensor(
+                out=psi[:], in0=trig[:, 1:2], scalar=pos_sin[:, 0:1], in1=psi[:], op0=ALU.mult, op1=ALU.add
+            )
+        half = small("half")
+        nc.vector.tensor_scalar(
+            out=half[:], in0=cw_c, scalar1=0.0, scalar2=-0.5, op0=ALU.is_ge, op1=ALU.add
+        )
+        phase = small("phase")
+        nc.vector.tensor_scalar(
+            out=phase[:], in0=psi[:], scalar1=half[:, 0:1], scalar2=1.0 / math.pi, op0=ALU.mult, op1=ALU.mult
+        )
 
         pb = keep.tile([128, N], F32)
-        for j in range(N // 512):
+
+        def spread_bias(j):
             ps = psum.tile([128, 512], F32, name="ps", tag="bank")
             nc.tensor.matmul(
                 out=ps[:], lhsT=ones[:], rhs=prow[:, 512 * j : 512 * (j + 1)], start=True, stop=True
             )
             nc.scalar.activation(
-                out=pb[:, 512 * j : 512 * (j + 1)], in_=ps[:], func=ACT.Copy,
-                bias=TURNS, scale=1.0 / (2.0 * math.pi),
+                out=pb[:, 512 * j : 512 * (j + 1)], in_=ps[:], func=ACT.Identity,
+                bias=phase[:, 0:1], scale=1.0 / TWO_PI,
             )
 
         lin = keep.tile([128, K], F32)
-        for c in range(0, K, 1536):
-            nc.scalar.activation(
-                out=lin[:, c : c + 1536], in_=x_sb[:, c : c + 1536], func=ACT.Identity, bias=p_c, scale=w_c
-            )
-
         per = keep.tile([128, N], F32)
 
         def plane(g, col):
@@ -157,38 +205,32 @@ def tile_time2vec_w_kernel(tc, x, W_words, W_scales, P, w, p, sine_w, cosine_w, 
                 return planes_b[4 * (g - 4) : 128, col : col + 512]
             return planes_c[4 * (j // 3) : 128, 512 * (j % 3) : 512 * (j % 3) + 512]
 
-        def front(acc, col):
-            u = work.tile([128, 512], F32, name="u", tag="u")
-            nc.vector.scalar_tensor_tensor(
-                out=u[:], in0=acc[:], scalar=1.0 / (2.0 * math.pi), in1=pb[:, col : col + 512],
-                op0=ALU.mult, op1=ALU.add,
-            )
-            ki = work.tile([128, 512], I32, name="ki", tag="ki")
-            nc.vector.tensor_copy(out=ki[:], in_=u[:])
-            f = work.tile([128, 512], F32, name="f", tag="f")
-            nc.vector.tensor_tensor(out=f[:], in0=u[:], in1=ki[:], op=ALU.subtract)
-            s = work.tile([128, 512], F32, name="s", tag="s")
-            nc.scalar.activation(out=s[:], in_=f[:], func=ACT.Sin, scale=2.0 * math.pi)
-            h = work.tile([128, 512], F32, name="h", tag="h")
-            nc.scalar.activation(out=h[:], in_=f[:], func=ACT.Sin, scale=math.pi)
-            nc.scalar.activation(out=h[:], in_=h[:], func=ACT.Square)
-            return u, f, s, h
-
-        def back(col, u, f, s, h):
-            nc.vector.tensor_scalar(
-                out=h[:], in0=h[:], scalar1=m2cw[:, 0:1], scalar2=cw_c, op0=ALU.mult, op1=ALU.add
-            )
-            if TEST_ROUND:
+        def epilogue(accs, cols):
+            turns = []
+            for acc, col in zip(accs, cols):
+                u = work.tile([128, 512], F32, name="u", tag="u", bufs=2 * BUNCH)
                 nc.vector.scalar_tensor_tensor(
-                    out=u[:], in0=u[:], scalar=-TURNS, in1=f[:], op0=ALU.add, op1=ALU.subtract
+                    out=u[:], in0=acc[:], scalar=1.0 / TWO_PI, in1=pb[:, col : col + 512],
+                    op0=ALU.mult, op1=ALU.add,
                 )
-                nc.vector.tensor_tensor(out=h[:], in0=h[:], in1=u[:], op=ALU.add)
-            nc.vector.scalar_tensor_tensor(
-                out=per[:, col : col + 512], in0=s[:], scalar=sw_c, in1=h[:], op0=ALU.mult, op1=ALU.add
-            )
+                turns.append(u)
+            whole = []
+            for u in turns:
+                ki = work.tile([128, 512], I32, name="ki", tag="ki")
+                nc.vector.tensor_copy(out=ki[:], in_=u[:])
+                whole.append(ki)
+            for u, ki in zip(turns, whole):
+                nc.vector.tensor_tensor(out=u[:], in0=u[:], in1=ki[:], op=ALU.subtract)
+            sines = []
+            for u in turns:
+                s = work.tile([128, 512], F32, name="s", tag="s")
+                nc.scalar.activation(out=s[:], in_=u[:], func=ACT.Sin, scale=TWO_PI)
+                sines.append(s)
+            for s, col in zip(sines, cols):
+                nc.scalar.activation(out=per[:, col : col + 512], in_=s[:], func=ACT.Copy, scale=amp[:, 0:1])
 
         i = 0
-        for c0, width in ROUNDS:
+        for n_round, (c0, width) in enumerate(ROUNDS):
             cols = list(range(c0, c0 + width, 512))
             accs = [psum.tile([128, 512], F32, name="acc", tag="bank") for col in cols]
             for g in range(GROUPS):
@@ -206,13 +248,14 @@ def tile_time2vec_w_kernel(tc, x, W_words, W_scales, P, w, p, sine_w, cosine_w, 
                 if i + W_BUFS < len(chunks):
                     load_chunk(i + W_BUFS)
                 i += 1
-            held = None
-            for acc, col in zip(accs, cols):
-                parts = front(acc, col)
-                if held is not None:
-                    back(*held)
-                held = (col,) + parts
-            back(*held)
+                if n_round == 0:
+                    spread_bias(g)
+                    nc.scalar.activation(
+                        out=lin[:, 512 * g : 512 * (g + 1)], in_=x_sb[:, 512 * g : 512 * (g + 1)],
+                        func=ACT.Identity, bias=p_c, scale=w_c,
+                    )
+            for first in range(0, len(cols), BUNCH):
+                epilogue(accs[first : first + BUNCH], cols[first : first + BUNCH])
 
         nc.sync.dma_start(out=out[:, 0:K], in_=lin[:])
         for c0, width in ROUNDS[:-1]:

@@ -22,7 +22,7 @@ FLOPS = 2 * B * K * N
 ROUNDS = ((0, 3072), (3072, 1536))
 W_MAX = 3072
 W_BUFS = 8
-BUNCH = 3
+BUNCH = 2
 NEWTON = 4
 TWO_PI = 2.0 * math.pi
 

@@ -53,10 +53,10 @@ def tile_time2vec_w_kernel(tc, x, W_words, W_scales, P, w, p, sine_w, cosine_w, 
         make_identity(nc, ident[:])
 
         for i, s in enumerate((w, p, sine_w, cosine_w)):
-            nc.scalar.dma_start(
+            nc.gpsimd.dma_start(
                 out=prow[0:1, N + 16 * i : N + 16 * i + 1], in_=s.rearrange("(o n) -> o n", o=1)
             )
-        nc.scalar.dma_start(out=prow[0:1, 0:N], in_=P.rearrange("(o n) -> o n", o=1))
+        nc.gpsimd.dma_start(out=prow[0:1, 0:N], in_=P.rearrange("(o n) -> o n", o=1))
 
         for planes, g0 in ((planes_a, 0), (planes_b, 4)):
             for q in range(4):

@@ -39,8 +39,6 @@ def tile_time2vec_w_kernel(tc, x, W_words, W_scales, P, w, p, sine_w, cosine_w, 
         x_sb = keep.tile([B, K], BF16, align_bytes=64)
         nc.sync.dma_start(out=x_sb[:], in_=x[:, :])
 
-        prow = keep.tile([128, N + 64], BF16)
-        nc.vector.memset(prow[:], 0.0)
         planes_a = keep.tile([128, N], U8, align_bytes=64)
         planes_b = keep.tile([128, N], U8, align_bytes=64)
         planes_c = keep.tile([128, N // 3], U8, align_bytes=64)
@@ -51,24 +49,14 @@ def tile_time2vec_w_kernel(tc, x, W_words, W_scales, P, w, p, sine_w, cosine_w, 
         nc.vector.memset(ones[:], 1.0)
         ident = keep.tile([128, 128], F32)
         make_identity(nc, ident[:])
+        prow = keep.tile([128, N + 64], BF16)
+        nc.gpsimd.memset(prow[:], 0.0)
 
         for i, s in enumerate((w, p, sine_w, cosine_w)):
             nc.gpsimd.dma_start(
                 out=prow[0:1, N + 16 * i : N + 16 * i + 1], in_=s.rearrange("(o n) -> o n", o=1)
             )
         nc.gpsimd.dma_start(out=prow[0:1, 0:N], in_=P.rearrange("(o n) -> o n", o=1))
-
-        for planes, g0 in ((planes_a, 0), (planes_b, 4)):
-            for q in range(4):
-                nc.sync.dma_start(
-                    out=planes[32 * q : 32 * q + 16, :].bitcast(I32),
-                    in_=W_scales[g0 : g0 + 4, 4 * q : 4 * q + 4, :].bitcast(I32),
-                )
-        for q in range(4):
-            nc.sync.dma_start(
-                out=planes_c[32 * q : 32 * q + 12, :].bitcast(I32),
-                in_=W_scales[8, 4 * q : 4 * q + 4, :].rearrange("r (k c) -> k r c", k=3).bitcast(I32),
-            )
 
         chunks = [(c0, width, g) for (c0, width) in ROUNDS for g in range(GROUPS)]
         w_tiles = {}
@@ -82,7 +70,25 @@ def tile_time2vec_w_kernel(tc, x, W_words, W_scales, P, w, p, sine_w, cosine_w, 
             )
             w_tiles[i] = wt
 
-        for i in range(W_BUFS):
+        def load_scales(planes, g0):
+            for q in range(4):
+                nc.sync.dma_start(
+                    out=planes[32 * q : 32 * q + 16, :].bitcast(I32),
+                    in_=W_scales[g0 : g0 + 4, 4 * q : 4 * q + 4, :].bitcast(I32),
+                )
+
+        load_chunk(0)
+        load_chunk(1)
+        load_scales(planes_a, 0)
+        load_chunk(2)
+        load_scales(planes_b, 4)
+        load_chunk(3)
+        for q in range(4):
+            nc.sync.dma_start(
+                out=planes_c[32 * q : 32 * q + 12, :].bitcast(I32),
+                in_=W_scales[8, 4 * q : 4 * q + 4, :].rearrange("r (k c) -> k r c", k=3).bitcast(I32),
+            )
+        for i in range(4, W_BUFS):
             load_chunk(i)
 
         xw = x_sb[:].bitcast(F32)

@@ -39,6 +39,10 @@ def tile_time2vec_w_kernel(tc, x, W_words, W_scales, P, w, p, sine_w, cosine_w, 
         x_sb = keep.tile([B, K], BF16, align_bytes=64)
         nc.sync.dma_start(out=x_sb[:], in_=x[:, :])
 
+        srow = keep.tile([128, 64], BF16)
+        nc.vector.memset(srow[:], 0.0)
+        for i, s in enumerate((w, p, sine_w, cosine_w)):
+            nc.scalar.dma_start(out=srow[0:1, 16 * i : 16 * i + 1], in_=s.rearrange("(o n) -> o n", o=1))
         planes_a = keep.tile([128, N], U8, align_bytes=64)
         planes_b = keep.tile([128, N], U8, align_bytes=64)
         planes_c = keep.tile([128, N // 3], U8, align_bytes=64)
@@ -49,13 +53,9 @@ def tile_time2vec_w_kernel(tc, x, W_words, W_scales, P, w, p, sine_w, cosine_w, 
         nc.vector.memset(ones[:], 1.0)
         ident = keep.tile([128, 128], F32)
         make_identity(nc, ident[:])
-        prow = keep.tile([128, N + 64], BF16)
-        nc.gpsimd.memset(prow[:], 0.0)
+        prow = keep.tile([128, N], BF16)
+        nc.vector.memset(prow[:].bitcast(I32), 0)
 
-        for i, s in enumerate((w, p, sine_w, cosine_w)):
-            nc.gpsimd.dma_start(
-                out=prow[0:1, N + 16 * i : N + 16 * i + 1], in_=s.rearrange("(o n) -> o n", o=1)
-            )
         nc.gpsimd.dma_start(out=prow[0:1, 0:N], in_=P.rearrange("(o n) -> o n", o=1))
 
         chunks = [(c0, width, g) for (c0, width) in ROUNDS for g in range(GROUPS)]
@@ -119,13 +119,23 @@ def tile_time2vec_w_kernel(tc, x, W_words, W_scales, P, w, p, sine_w, cosine_w, 
         quantise(*pairs[-1])
 
         ps = psum.tile([128, 512], F32, name="ps", tag="bank")
-        nc.tensor.matmul(out=ps[:, 0:64], lhsT=ones[:], rhs=prow[:, N : N + 64], start=True, stop=True)
+        nc.tensor.matmul(out=ps[:, 0:64], lhsT=ones[:], rhs=srow[:], start=True, stop=True)
         sc4 = keep.tile([128, 4], F32)
         nc.vector.tensor_copy(out=sc4[:], in_=ps[:, 0:64:16])
         w_c = sc4[:, 0:1]
         p_c = sc4[:, 1:2]
         sw_c = sc4[:, 2:3]
         cw_c = sc4[:, 3:4]
+
+        pb = keep.tile([128, N], F32)
+        for j in range(N // 512):
+            ps = psum.tile([128, 512], F32, name="ps", tag="bank")
+            nc.tensor.matmul(
+                out=ps[:], lhsT=ones[:], rhs=prow[:, 512 * j : 512 * (j + 1)], start=True, stop=True
+            )
+            nc.scalar.activation(
+                out=pb[:, 512 * j : 512 * (j + 1)], in_=ps[:], func=ACT.Copy, scale=1.0 / TWO_PI
+            )
 
         def small(name, width=1):
             return keep.tile([128, width], F32, name=name)
@@ -188,16 +198,9 @@ def tile_time2vec_w_kernel(tc, x, W_words, W_scales, P, w, p, sine_w, cosine_w, 
             out=phase[:], in0=psi[:], scalar1=half[:, 0:1], scalar2=1.0 / math.pi, op0=ALU.mult, op1=ALU.mult
         )
 
-        pb = keep.tile([128, N], F32)
-
-        def spread_bias(j):
-            ps = psum.tile([128, 512], F32, name="ps", tag="bank")
-            nc.tensor.matmul(
-                out=ps[:], lhsT=ones[:], rhs=prow[:, 512 * j : 512 * (j + 1)], start=True, stop=True
-            )
-            nc.scalar.activation(
-                out=pb[:, 512 * j : 512 * (j + 1)], in_=ps[:], func=ACT.Identity,
-                bias=phase[:, 0:1], scale=1.0 / TWO_PI,
+        for c0, width in ROUNDS:
+            nc.vector.tensor_scalar_add(
+                out=pb[:, c0 : c0 + width], in0=pb[:, c0 : c0 + width], scalar1=phase[:, 0:1]
             )
 
         lin = keep.tile([128, K], F32)
@@ -255,7 +258,6 @@ def tile_time2vec_w_kernel(tc, x, W_words, W_scales, P, w, p, sine_w, cosine_w, 
                     load_chunk(i + W_BUFS)
                 i += 1
                 if n_round == 0:
-                    spread_bias(g)
                     nc.scalar.activation(
                         out=lin[:, 512 * g : 512 * (g + 1)], in_=x_sb[:, 512 * g : 512 * (g + 1)],
                         func=ACT.Identity, bias=p_c, scale=w_c,

@@ -19,7 +19,7 @@ N = 4608
 GROUPS = K // 512
 FLOPS = 2 * B * K * N
 
-ROUNDS = ((0, 3072), (3072, 1536))
+ROUNDS = ((0, 3072), (3072, 1024), (4096, 512))
 W_MAX = 3072
 W_BUFS = 8
 BUNCH = 2
@@ -58,15 +58,19 @@ def tile_time2vec_w_kernel(tc, x, W_words, W_scales, P, w, p, sine_w, cosine_w, 
 
         nc.gpsimd.dma_start(out=prow[0:1, 0:N], in_=P.rearrange("(o n) -> o n", o=1))
 
-        chunks = [(c0, width, g) for (c0, width) in ROUNDS for g in range(GROUPS)]
+        chunks = []
+        for c0, width in ROUNDS:
+            per_tile = W_MAX // width
+            for g in range(0, GROUPS, per_tile):
+                chunks.append((c0, width, g, min(per_tile, GROUPS - g)))
         w_tiles = {}
 
         def load_chunk(i):
-            c0, width, g = chunks[i]
+            c0, width, g, ng = chunks[i]
             wt = wpool.tile([128, 4 * W_MAX], U8, name="wt", tag="wt", align_bytes=64)
             nc.sync.dma_start(
-                out=wt[:, 0 : 4 * width].bitcast(I32),
-                in_=W_words[g].rearrange("p n t -> p (n t)")[:, 4 * c0 : 4 * (c0 + width)].bitcast(I32),
+                out=wt[:, 0 : 4 * width * ng].rearrange("p (g c) -> p g c", g=ng).bitcast(I32),
+                in_=W_words[g : g + ng].rearrange("g p n t -> p g (n t)")[:, :, 4 * c0 : 4 * (c0 + width)].bitcast(I32),
             )
             w_tiles[i] = wt
 
@@ -244,28 +248,34 @@ def tile_time2vec_w_kernel(tc, x, W_words, W_scales, P, w, p, sine_w, cosine_w, 
             accs = [psum.tile([128, 512], F32, name="acc", tag="bank") for col in cols]
             for g in range(GROUPS):
                 wt = w_tiles[i]
+                first_g, ng = chunks[i][2:]
+                base = 4 * width * (g - first_g)
                 for acc, col in zip(accs, cols):
                     nc.tensor.matmul_mx(
                         out=acc[:],
                         lhsT=xcodes[:, B * g : B * (g + 1)].bitcast(FP8X4),
                         lhsT_scale=xscales[:, B * g : B * (g + 1)],
-                        rhs=wt[:, 4 * (col - c0) : 4 * (col - c0) + 2048].bitcast(FP8X4),
+                        rhs=wt[:, base + 4 * (col - c0) : base + 4 * (col - c0) + 2048].bitcast(FP8X4),
                         rhs_scale=plane(g, col),
                         start=(g == 0),
                         stop=(g == GROUPS - 1),
                     )
-                if i + W_BUFS < len(chunks):
-                    load_chunk(i + W_BUFS)
-                i += 1
+                if g == first_g + ng - 1:
+                    if i + W_BUFS < len(chunks):
+                        load_chunk(i + W_BUFS)
+                    i += 1
                 if n_round == 0:
                     nc.scalar.activation(
                         out=lin[:, 512 * g : 512 * (g + 1)], in_=x_sb[:, 512 * g : 512 * (g + 1)],
                         func=ACT.Identity, bias=p_c, scale=w_c,
                     )
+            if n_round == 0:
+                nc.gpsimd.dma_start(out=out[0:108, 0:K], in_=lin[0:108, :], max_dma_last_dim=2 * K)
             for first in range(0, len(cols), BUNCH):
                 epilogue(accs[first : first + BUNCH], cols[first : first + BUNCH])
 
-        nc.sync.dma_start(out=out[:, 0:K], in_=lin[:])
+        nc.sync.dma_start(out=out[108:124, 0:K], in_=lin[108:124, :])
+        nc.sync.dma_start(out=out[124:128, 0:K], in_=lin[124:128, :])
         for c0, width in ROUNDS[:-1]:
             nc.sync.dma_start(out=out[:, K + c0 : K + c0 + width], in_=per[:, c0 : c0 + width])
         c0, width = ROUNDS[-1]

@@ -270,12 +270,13 @@ def tile_time2vec_w_kernel(tc, x, W_words, W_scales, P, w, p, sine_w, cosine_w, 
                         func=ACT.Identity, bias=p_c, scale=w_c,
                     )
             if n_round == 0:
-                nc.gpsimd.dma_start(out=out[0:108, 0:K], in_=lin[0:108, :], max_dma_last_dim=2 * K)
+                nc.gpsimd.dma_start(out=out[124:128, 0:K], in_=lin[124:128, :], max_dma_last_dim=2 * K)
+                nc.gpsimd.dma_start(out=out[0:108, 0:3840], in_=lin[0:108, 0:3840], max_dma_last_dim=2 * 3840)
             for first in range(0, len(cols), BUNCH):
                 epilogue(accs[first : first + BUNCH], cols[first : first + BUNCH])
 
         nc.sync.dma_start(out=out[108:124, 0:K], in_=lin[108:124, :])
-        nc.sync.dma_start(out=out[124:128, 0:K], in_=lin[124:128, :])
+        nc.sync.dma_start(out=out[0:108, 3840:K], in_=lin[0:108, 3840:K])
         for c0, width in ROUNDS[:-1]:
             nc.sync.dma_start(out=out[:, K + c0 : K + c0 + width], in_=per[:, c0 : c0 + width])
         c0, width = ROUNDS[-1]

@@ -23,6 +23,7 @@ ROUNDS = ((0, 3072), (3072, 1024), (4096, 512))
 W_MAX = 3072
 W_BUFS = 8
 BUNCH = 2
+EARLY = 2560
 NEWTON = 4
 TWO_PI = 2.0 * math.pi
 
@@ -81,18 +82,17 @@ def tile_time2vec_w_kernel(tc, x, W_words, W_scales, P, w, p, sine_w, cosine_w, 
                     in_=W_scales[g0 : g0 + 4, 4 * q : 4 * q + 4, :].bitcast(I32),
                 )
 
+        load_scales(planes_a, 0)
         load_chunk(0)
         load_chunk(1)
-        load_scales(planes_a, 0)
         load_chunk(2)
         load_scales(planes_b, 4)
-        load_chunk(3)
         for q in range(4):
             nc.sync.dma_start(
                 out=planes_c[32 * q : 32 * q + 12, :].bitcast(I32),
                 in_=W_scales[8, 4 * q : 4 * q + 4, :].rearrange("r (k c) -> k r c", k=3).bitcast(I32),
             )
-        for i in range(4, W_BUFS):
+        for i in range(3, W_BUFS):
             load_chunk(i)
 
         xw = x_sb[:].bitcast(F32)
@@ -130,6 +130,17 @@ def tile_time2vec_w_kernel(tc, x, W_words, W_scales, P, w, p, sine_w, cosine_w, 
         p_c = sc4[:, 1:2]
         sw_c = sc4[:, 2:3]
         cw_c = sc4[:, 3:4]
+
+        lin = keep.tile([128, K], F32)
+
+        def linear(first, last):
+            nc.scalar.activation(
+                out=lin[:, first:last], in_=x_sb[:, first:last], func=ACT.Identity, bias=p_c, scale=w_c
+            )
+
+        linear(0, EARLY)
+        for r0, r1 in ((124, 128), (0, 108)):
+            nc.gpsimd.dma_start(out=out[r0:r1, 0:EARLY], in_=lin[r0:r1, 0:EARLY], max_dma_last_dim=2 * EARLY)
 
         pb = keep.tile([128, N], F32)
         for j in range(N // 512):
@@ -207,7 +218,6 @@ def tile_time2vec_w_kernel(tc, x, W_words, W_scales, P, w, p, sine_w, cosine_w, 
                 out=pb[:, c0 : c0 + width], in0=pb[:, c0 : c0 + width], scalar1=phase[:, 0:1]
             )
 
-        lin = keep.tile([128, K], F32)
         per = keep.tile([128, N], F32)
 
         def plane(g, col):
@@ -265,18 +275,13 @@ def tile_time2vec_w_kernel(tc, x, W_words, W_scales, P, w, p, sine_w, cosine_w, 
                         load_chunk(i + W_BUFS)
                     i += 1
                 if n_round == 0:
-                    nc.scalar.activation(
-                        out=lin[:, 512 * g : 512 * (g + 1)], in_=x_sb[:, 512 * g : 512 * (g + 1)],
-                        func=ACT.Identity, bias=p_c, scale=w_c,
-                    )
-            if n_round == 0:
-                nc.gpsimd.dma_start(out=out[124:128, 0:K], in_=lin[124:128, :], max_dma_last_dim=2 * K)
-                nc.gpsimd.dma_start(out=out[0:108, 0:3840], in_=lin[0:108, 0:3840], max_dma_last_dim=2 * 3840)
+                    if 512 * g >= EARLY:
+                        linear(512 * g, 512 * (g + 1))
             for first in range(0, len(cols), BUNCH):
                 epilogue(accs[first : first + BUNCH], cols[first : first + BUNCH])
 
-        nc.sync.dma_start(out=out[108:124, 0:K], in_=lin[108:124, :])
-        nc.sync.dma_start(out=out[0:108, 3840:K], in_=lin[0:108, 3840:K])
+        nc.sync.dma_start(out=out[108:124, 0:EARLY], in_=lin[108:124, 0:EARLY])
+        nc.sync.dma_start(out=out[:, EARLY:K], in_=lin[:, EARLY:K])
         for c0, width in ROUNDS[:-1]:
             nc.sync.dma_start(out=out[:, K + c0 : K + c0 + width], in_=per[:, c0 : c0 + width])
         c0, width = ROUNDS[-1]

import math
from contextlib import ExitStack

import concourse.mybir as mybir
from concourse.masks import make_identity

F32 = mybir.dt.float32
BF16 = mybir.dt.bfloat16
I32 = mybir.dt.int32
U32 = mybir.dt.uint32
U8 = mybir.dt.uint8
FP8X4 = mybir.dt.float8_e4m3fn_x4
ALU = mybir.AluOpType
ACT = mybir.ActivationFunctionType

B = 128
K = 4608
N = 4608
GROUPS = K // 512
FLOPS = 2 * B * K * N

ROUNDS = ((0, 3072), (3072, 1024), (4096, 512))
W_MAX = 3072
W_BUFS = 8
BUNCH = 2
EARLY = 2560
NEWTON = 4
TWO_PI = 2.0 * math.pi


def tile_time2vec_w_kernel(tc, x, W_words, W_scales, P, w, p, sine_w, cosine_w, out):
    nc = tc.nc
    with ExitStack() as ctx:
        keep = ctx.enter_context(tc.tile_pool(name="keep", bufs=1))
        wpool = ctx.enter_context(tc.tile_pool(name="wpool", bufs=W_BUFS))
        work = ctx.enter_context(tc.tile_pool(name="work", bufs=4))
        psum = ctx.enter_context(tc.psum_pool(name="psum", bufs=8))
        ctx.enter_context(tc.manual_schedule())

        x_sb = keep.tile([B, K], BF16, align_bytes=64)
        nc.sync.dma_start(out=x_sb[:], in_=x[:, :])

        srow = keep.tile([128, 64], BF16)
        nc.vector.memset(srow[:], 0.0)
        for i, s in enumerate((w, p, sine_w, cosine_w)):
            nc.scalar.dma_start(out=srow[0:1, 16 * i : 16 * i + 1], in_=s.rearrange("(o n) -> o n", o=1))
        planes_a = keep.tile([128, N], U8, align_bytes=64)
        planes_b = keep.tile([128, N], U8, align_bytes=64)
        planes_c = keep.tile([128, N // 3], U8, align_bytes=64)
        nc.vector.memset(planes_a[:].bitcast(I32), 0)
        nc.vector.memset(planes_b[:].bitcast(I32), 0)
        nc.vector.memset(planes_c[:].bitcast(I32), 0)
        ones = keep.tile([128, 128], BF16)
        nc.vector.memset(ones[:], 1.0)
        ident = keep.tile([128, 128], F32)
        make_identity(nc, ident[:])
        prow = keep.tile([128, N], BF16)
        nc.vector.memset(prow[:].bitcast(I32), 0)

        nc.gpsimd.dma_start(out=prow[0:1, 0:N], in_=P.rearrange("(o n) -> o n", o=1))

        chunks = []
        for c0, width in ROUNDS:
            per_tile = W_MAX // width
            for g in range(0, GROUPS, per_tile):
                chunks.append((c0, width, g, min(per_tile, GROUPS - g)))
        w_tiles = {}

        def load_chunk(i):
            c0, width, g, ng = chunks[i]
            wt = wpool.tile([128, 4 * W_MAX], U8, name="wt", tag="wt", align_bytes=64)
            nc.sync.dma_start(
                out=wt[:, 0 : 4 * width * ng].rearrange("p (g c) -> p g c", g=ng).bitcast(I32),
                in_=W_words[g : g + ng].rearrange("g p n t -> p g (n t)")[:, :, 4 * c0 : 4 * (c0 + width)].bitcast(I32),
            )
            w_tiles[i] = wt

        def load_scales(planes, g0):
            for q in range(4):
                nc.sync.dma_start(
                    out=planes[32 * q : 32 * q + 16, :].bitcast(I32),
                    in_=W_scales[g0 : g0 + 4, 4 * q : 4 * q + 4, :].bitcast(I32),
                )

        load_scales(planes_a, 0)
        load_chunk(0)
        load_chunk(1)
        load_chunk(2)
        load_scales(planes_b, 4)
        for q in range(4):
            nc.sync.dma_start(
                out=planes_c[32 * q : 32 * q + 12, :].bitcast(I32),
                in_=W_scales[8, 4 * q : 4 * q + 4, :].rearrange("r (k c) -> k r c", k=3).bitcast(I32),
            )
        for i in range(3, W_BUFS):
            load_chunk(i)

        xw = x_sb[:].bitcast(F32)
        grouped = keep.tile([128, K], BF16, align_bytes=64)
        g32 = grouped[:].bitcast(F32).rearrange("p (g b u) -> p g b u", g=GROUPS, b=B, u=2)
        xcodes = keep.tile([128, GROUPS * B], U32, align_bytes=64)
        xscales = keep.tile([128, GROUPS * B], U8, align_bytes=64)
        pairs = [(g0, min(2, GROUPS - g0)) for g0 in range(0, GROUPS, 2)]

        def quantise(g0, ng):
            nc.vector.quantize_mx(
                out=xcodes[:, B * g0 : B * (g0 + ng)].bitcast(FP8X4),
                scales=xscales[:, B * g0 : B * (g0 + ng)],
                in_=grouped[:, 512 * g0 : 512 * (g0 + ng)],
            )

        for n_pair, (g0, ng) in enumerate(pairs):
            xt = psum.tile([128, 2, 2, B], F32, name="xt", tag="bank")
            for j in range(ng):
                for u in range(2):
                    g = g0 + j
                    nc.tensor.transpose(xt[:, j, u, :], xw[:, 256 * g + u : 256 * (g + 1) : 2], ident[:])
            nc.vector.tensor_copy(
                out=g32[:, g0 : g0 + ng], in_=xt[:, 0:ng].rearrange("p g u b -> p g b u")
            )
            if n_pair > 0:
                quantise(*pairs[n_pair - 1])
        quantise(*pairs[-1])

        ps = psum.tile([128, 512], F32, name="ps", tag="bank")
        nc.tensor.matmul(out=ps[:, 0:64], lhsT=ones[:], rhs=srow[:], start=True, stop=True)
        sc4 = keep.tile([128, 4], F32)
        nc.vector.tensor_copy(out=sc4[:], in_=ps[:, 0:64:16])
        w_c = sc4[:, 0:1]
        p_c = sc4[:, 1:2]
        sw_c = sc4[:, 2:3]
        cw_c = sc4[:, 3:4]

        lin = keep.tile([128, K], F32)

        def linear(first, last):
            nc.scalar.activation(
                out=lin[:, first:last], in_=x_sb[:, first:last], func=ACT.Identity, bias=p_c, scale=w_c
            )

        linear(0, EARLY)
        for r0, r1 in ((124, 128), (0, 108)):
            nc.gpsimd.dma_start(out=out[r0:r1, 0:EARLY], in_=lin[r0:r1, 0:EARLY], max_dma_last_dim=2 * EARLY)

        pb = keep.tile([128, N], F32)
        for j in range(N // 512):
            ps = psum.tile([128, 512], F32, name="ps", tag="bank")
            nc.tensor.matmul(
                out=ps[:], lhsT=ones[:], rhs=prow[:, 512 * j : 512 * (j + 1)], start=True, stop=True
            )
            nc.scalar.activation(
                out=pb[:, 512 * j : 512 * (j + 1)], in_=ps[:], func=ACT.Copy, scale=1.0 / TWO_PI
            )

        def small(name, width=1):
            return keep.tile([128, width], F32, name=name)

        mag = small("mag", 2)
        nc.vector.scalar_tensor_tensor(
            out=mag[:], in0=sc4[:, 2:4], scalar=-1.0, in1=sc4[:, 2:4], op0=ALU.mult, op1=ALU.max
        )
        big = small("big")
        nc.vector.scalar_tensor_tensor(
            out=big[:], in0=mag[:, 0:1], scalar=1e-30, in1=mag[:, 1:2], op0=ALU.max, op1=ALU.max
        )
        rbig = small("rbig")
        nc.vector.reciprocal(out=rbig[:], in_=big[:])
        vec = small("vec", 2)
        nc.vector.tensor_scalar_mul(out=vec[:, 0:1], in0=sw_c, scalar1=rbig[:, 0:1])
        nc.vector.tensor_scalar_mul(out=vec[:, 1:2], in0=mag[:, 1:2], scalar1=rbig[:, 0:1])
        sq = small("sq", 2)
        nc.vector.tensor_tensor(out=sq[:], in0=vec[:], in1=vec[:], op=ALU.mult)
        n2 = small("n2")
        nc.vector.tensor_scalar(
            out=n2[:], in0=sq[:, 0:1], scalar1=sq[:, 1:2], scalar2=0.25, op0=ALU.add, op1=ALU.max
        )
        root = small("root")
        nc.scalar.activation(out=root[:], in_=n2[:], func=ACT.Sqrt)
        rroot = small("rroot")
        nc.vector.reciprocal(out=rroot[:], in_=root[:])
        twice = small("twice")
        nc.vector.tensor_scalar(
            out=twice[:], in0=n2[:], scalar1=rroot[:, 0:1], scalar2=root[:, 0:1], op0=ALU.mult, op1=ALU.add
        )
        amp = small("amp")
        nc.vector.tensor_scalar(
            out=amp[:], in0=twice[:], scalar1=0.5, scalar2=big[:, 0:1], op0=ALU.mult, op1=ALU.mult
        )
        neg_cos = small("neg_cos")
        nc.vector.tensor_scalar(
            out=neg_cos[:], in0=vec[:, 0:1], scalar1=rroot[:, 0:1], scalar2=-1.0, op0=ALU.mult, op1=ALU.mult
        )
        pos_sin = small("pos_sin")
        nc.vector.tensor_scalar_mul(out=pos_sin[:], in0=vec[:, 1:2], scalar1=rroot[:, 0:1])
        psi = small("psi")
        nc.vector.memset(psi[:], math.pi / 2.0)
        trig = small("trig", 2)
        for step in range(NEWTON):
            nc.scalar.activation(out=trig[:, 0:1], in_=psi[:], func=ACT.Sin)
            nc.scalar.activation(out=trig[:, 1:2], in_=psi[:], func=ACT.Sin, bias=math.pi / 2.0, scale=-1.0)
            nc.vector.scalar_tensor_tensor(
                out=psi[:], in0=trig[:, 0:1], scalar=neg_cos[:, 0:1], in1=psi[:], op0=ALU.mult, op1=ALU.add
            )
            nc.vector.scalar_tensor_tensor(
                out=psi[:], in0=trig[:, 1:2], scalar=pos_sin[:, 0:1], in1=psi[:], op0=ALU.mult, op1=ALU.add
            )
        half = small("half")
        nc.vector.tensor_scalar(
            out=half[:], in0=cw_c, scalar1=0.0, scalar2=-0.5, op0=ALU.is_ge, op1=ALU.add
        )
        phase = small("phase")
        nc.vector.tensor_scalar(
            out=phase[:], in0=psi[:], scalar1=half[:, 0:1], scalar2=1.0 / math.pi, op0=ALU.mult, op1=ALU.mult
        )

        for c0, width in ROUNDS:
            nc.vector.tensor_scalar_add(
                out=pb[:, c0 : c0 + width], in0=pb[:, c0 : c0 + width], scalar1=phase[:, 0:1]
            )

        per = keep.tile([128, N], F32)

        def plane(g, col):
            j = col // 512
            if g < 4:
                return planes_a[4 * g : 128, col : col + 512]
            if g < 8:
                return planes_b[4 * (g - 4) : 128, col : col + 512]
            return planes_c[4 * (j // 3) : 128, 512 * (j % 3) : 512 * (j % 3) + 512]

        def epilogue(accs, cols):
            turns = []
            for acc, col in zip(accs, cols):
                u = work.tile([128, 512], F32, name="u", tag="u", bufs=2 * BUNCH)
                nc.vector.scalar_tensor_tensor(
                    out=u[:], in0=acc[:], scalar=1.0 / TWO_PI, in1=pb[:, col : col + 512],
                    op0=ALU.mult, op1=ALU.add,
                )
                turns.append(u)
            whole = []
            for u in turns:
                ki = work.tile([128, 512], I32, name="ki", tag="ki")
                nc.vector.tensor_copy(out=ki[:], in_=u[:])
                whole.append(ki)
            for u, ki in zip(turns, whole):
                nc.vector.tensor_tensor(out=u[:], in0=u[:], in1=ki[:], op=ALU.subtract)
            sines = []
            for u in turns:
                s = work.tile([128, 512], F32, name="s", tag="s")
                nc.scalar.activation(out=s[:], in_=u[:], func=ACT.Sin, scale=TWO_PI)
                sines.append(s)
            for s, col in zip(sines, cols):
                nc.scalar.activation(out=per[:, col : col + 512], in_=s[:], func=ACT.Copy, scale=amp[:, 0:1])

        i = 0
        for n_round, (c0, width) in enumerate(ROUNDS):
            cols = list(range(c0, c0 + width, 512))
            accs = [psum.tile([128, 512], F32, name="acc", tag="bank") for col in cols]
            for g in range(GROUPS):
                wt = w_tiles[i]
                first_g, ng = chunks[i][2:]
                base = 4 * width * (g - first_g)
                for acc, col in zip(accs, cols):
                    nc.tensor.matmul_mx(
                        out=acc[:],
                        lhsT=xcodes[:, B * g : B * (g + 1)].bitcast(FP8X4),
                        lhsT_scale=xscales[:, B * g : B * (g + 1)],
                        rhs=wt[:, base + 4 * (col - c0) : base + 4 * (col - c0) + 2048].bitcast(FP8X4),
                        rhs_scale=plane(g, col),
                        start=(g == 0),
                        stop=(g == GROUPS - 1),
                    )
                if g == first_g + ng - 1:
                    if i + W_BUFS < len(chunks):
                        load_chunk(i + W_BUFS)
                    i += 1
                if n_round == 0:
                    if 512 * g >= EARLY:
                        linear(512 * g, 512 * (g + 1))
            for first in range(0, len(cols), BUNCH):
                epilogue(accs[first : first + BUNCH], cols[first : first + BUNCH])

        nc.sync.dma_start(out=out[108:124, 0:EARLY], in_=lin[108:124, 0:EARLY])
        nc.sync.dma_start(out=out[:, EARLY:K], in_=lin[:, EARLY:K])
        for c0, width in ROUNDS[:-1]:
            nc.sync.dma_start(out=out[:, K + c0 : K + c0 + width], in_=per[:, c0 : c0 + width])
        c0, width = ROUNDS[-1]
        for col in range(c0, c0 + width, 512):
            nc.sync.dma_start(out=out[:, K + col : K + col + 512], in_=per[:, col : col + 512])
